import numpy as np
import ml_dtypes


def mxq(x, axis, fmt="e4m3"):
    dtype, down = {"e4m3": (ml_dtypes.float8_e4m3fn, 7), "e5m2": (ml_dtypes.float8_e5m2, 14)}[fmt]
    v = np.moveaxis(np.asarray(x, np.float32).astype(ml_dtypes.bfloat16).astype(np.float64), axis, -1)
    blocks = v.reshape(v.shape[:-1] + (-1, 32))
    amax = np.abs(blocks).max(-1, keepdims=True)
    byte = np.maximum(np.where(amax > 0, np.frexp(amax)[1] - 1 + 127, 0) - down, 1)
    scale = np.exp2(byte - 127.0)
    codes = (blocks / scale).astype(np.float32).astype(dtype).astype(np.float64)
    return np.moveaxis((codes * scale).reshape(v.shape), -1, axis)


WIDE = False


def mx_kscale(k):
    if not WIDE:
        return np.ones(k)
    levels = np.array([10, -10, 5, -5, 0])
    if k % 512:
        return np.exp2(np.random.permutation(np.resize(levels, k // 32))).repeat(32)
    a = np.empty((k // 512, 16))
    for p in range(k // 512):
        a[p, :8] = np.random.permutation(np.resize(levels, 8))
        for g in range(8):
            far = levels[np.abs(levels - a[p, g]) >= 10]
            a[p, g + 8] = far[np.random.randint(len(far))]
    return np.exp2(a.ravel()).repeat(32)


BF16 = ml_dtypes.bfloat16


def bf(x):
    return np.asarray(x, np.float32).astype(BF16)


def f64(x):
    return np.asarray(x).astype(np.float64)


B, N, D, P, Z = 1, 128, 1024, 511, 32
P1 = P + 1


def leaky_draw(shape):
    g = np.random.standard_normal(shape)
    return np.where(g > 0.0, g, 0.1 * g)


def with_ones(v):
    return np.concatenate([v, np.ones(v.shape[:-1] + (1,))], axis=-1)


def setup_inputs():
    s, u = mx_kscale(P1), mx_kscale(P1)
    s, u = s / s[-1], u / u[-1]
    return {"xp": bf(leaky_draw((B, N, P)) * s[:P]),
            "yp": bf(leaky_draw((B, N, P)) / u[:P]),
            "w": bf(np.random.standard_normal((B, Z, P1, P1)) * 0.36 / np.sqrt(P1) / s[:, None] * u)}


def reference(xp, yp, w):
    x1 = mxq(with_ones(f64(xp)), 2, "e4m3")
    y1 = mxq(with_ones(f64(yp)), 2, "e4m3")
    t = x1[:, None] @ mxq(f64(w), 2, "e4m3")
    sc = mxq(t, 3, "e4m3") @ y1.transpose(0, 2, 1)[:, None]
    return sc.transpose(0, 2, 3, 1)

@@ -1,0 +1,192 @@
+from contextlib import ExitStack
+
+import concourse.mybir as mybir
+from concourse.masks import make_identity
+
+F32 = mybir.dt.float32
+BF16 = mybir.dt.bfloat16
+U32 = mybir.dt.uint32
+U8 = mybir.dt.uint8
+FP8X4 = mybir.dt.float8_e4m3fn_x4
+
+P = 128
+K = 512
+Z = 32
+ZG = 4
+BANK_DT = F32
+
+FLOPS = 2 * P * K * K * Z + 2 * P * P * K * Z
+
+A_V = 20
+R2_ON_V = (6,)
+PIECES = [(ZG * g, ZG) for g in range(Z // ZG - 1)] + [(28, 2), (30, 1), (31, 1)]
+Y_CUTS = (0, 32, 64, 96, 128)
+
+
+def tile_span2oscorer_pa_kernel(tc, xp, yp, w, out):
+    nc = tc.nc
+    with ExitStack() as ctx:
+        const = ctx.enter_context(tc.tile_pool(name="const", bufs=1))
+        rawp = ctx.enter_context(tc.tile_pool(name="rawp", bufs=Z))
+        grp = ctx.enter_context(tc.tile_pool(name="grp", bufs=3))
+        wq = ctx.enter_context(tc.tile_pool(name="wq", bufs=3))
+        tq = ctx.enter_context(tc.tile_pool(name="tq", bufs=2))
+        ps_head = ctx.enter_context(tc.psum_pool(name="ps_head", bufs=2))
+        ps1 = ctx.enter_context(tc.psum_pool(name="ps1", bufs=3))
+        ps2 = ctx.enter_context(tc.psum_pool(name="ps2", bufs=2))
+        ctx.enter_context(tc.manual_schedule())
+
+        x_sb = const.tile([P, K + 8], BF16, name="x_sb")
+        y_sb = const.tile([P, K + 8], BF16, name="y_sb")
+        nc.sync.dma_start(out=x_sb[:, 1:K], in_=xp[0])
+        nc.sync.dma_start(out=y_sb[:, 1:K], in_=yp[0])
+        nc.vector.memset(x_sb[:, K : K + 8], 1.0)
+        nc.vector.memset(y_sb[:, K : K + 8], 1.0)
+        raws = []
+        for z in range(Z):
+            raw = rawp.tile([P, 4, K], BF16, name="raw")
+            src = w[0, z].rearrange("(p t) j -> p t j", t=4)
+            if z < 1:
+                nc.sync.dma_start(out=raw[:, :, 0 : 16 * A_V], in_=src[:, :, 0 : 16 * A_V])
+                nc.sync.dma_start(out=raw[:, :, 16 * A_V : K], in_=src[:, :, 16 * A_V : K])
+            else:
+                nc.sync.dma_start(out=raw[:], in_=src)
+            raws.append(raw)
+
+        ident = const.tile([P, P], BF16, name="ident")
+        make_identity(nc, ident[:])
+
+        x_slot = const.tile([P, 4, P], BF16, name="x_slot")
+        y_slot = const.tile([P, 4, P], BF16, name="y_slot")
+        nc.vector.tensor_copy(out=x_slot[:], in_=x_sb[:, 1 : K + 1].rearrange("r (p t) -> r t p", t=4))
+        nc.vector.tensor_copy(
+            out=y_slot[:].rearrange("r s (a i) -> r s a i", i=4),
+            in_=y_sb[:, 1 : K + 1].rearrange("r (a s i) -> r s a i", s=4, i=4),
+        )
+        x_grp = const.tile([P, P, 4], BF16, name="x_grp", align_bytes=64)
+        y_grp = const.tile([P, P, 4], BF16, name="y_grp", align_bytes=64)
+        for slot, grouped in ((x_slot, x_grp), (y_slot, y_grp)):
+            turned = ps_head.tile([P, 4, P], BF16, name="turned")
+            for t in range(4):
+                nc.tensor.transpose(turned[:, t, :], slot[:, t, :], ident[:])
+            nc.scalar.copy(out=grouped[:], in_=turned[:].rearrange("p t r -> p r t"))
+        x_codes = const.tile([P, P], U32, name="x_codes", align_bytes=64)
+        x_scales = const.tile([P, P], U8, name="x_scales", align_bytes=64)
+        y_codes = const.tile([P, P], U32, name="y_codes", align_bytes=64)
+        y_scales = const.tile([P, P], U8, name="y_scales", align_bytes=64)
+
+        out_sb = const.tile([P, P, Z], F32, name="out_sb")
+
+        w_grps = {}
+        w_codes = {}
+        w_scales = {}
+        banks1 = {}
+        t_grps = {}
+        t_codes = {}
+        t_scales = {}
+        banks2 = {}
+
+        def interleave(z):
+            g = grp.tile([P, 4 * K], BF16, name="w_grp", align_bytes=64)
+            w_grps[z] = g
+            dst = g[:].rearrange("p (s a i t) -> p a s i t", s=4, a=32, i=4, t=4)
+            src = raws[z][:].rearrange("p t (a s i) -> p a s i t", a=32, s=4, i=4)
+            nc.scalar.copy(out=dst[:, A_V:32], in_=src[:, A_V:32])
+            nc.vector.tensor_copy(out=dst[:, 0:A_V], in_=src[:, 0:A_V])
+
+        def quantize_w(z):
+            c = wq.tile([P, K], U32, name="w_code", align_bytes=64)
+            s = wq.tile([P, K], U8, name="w_scale", align_bytes=64)
+            w_codes[z] = c
+            w_scales[z] = s
+            nc.vector.quantize_mx(out=c[:].bitcast(FP8X4), scales=s[:], in_=w_grps[z][:])
+
+        def stage1(z):
+            b = ps1.tile([P, 4, P], BANK_DT, name="bank1")
+            banks1[z] = b
+            for s in range(4):
+                cols = slice(s * P, (s + 1) * P)
+                nc.tensor.matmul_mx(
+                    out=b[:, s, :],
+                    lhsT=w_codes[z][:, cols].bitcast(FP8X4),
+                    lhsT_scale=w_scales[z][:, cols],
+                    rhs=x_codes[:].bitcast(FP8X4),
+                    rhs_scale=x_scales[:],
+                    start=True,
+                    stop=True,
+                )
+
+        def read1(z):
+            g = z // ZG
+            if z % ZG == 0:
+                t_grps[g] = tq.tile([P, ZG, P, 4], BF16, name="t_grp", align_bytes=64)
+                t_codes[g] = tq.tile([P, ZG * P], U32, name="t_code", align_bytes=64)
+                t_scales[g] = tq.tile([P, ZG * P], U8, name="t_scale", align_bytes=64)
+            nc.scalar.copy(out=t_grps[g][:, z % ZG], in_=banks1[z][:].rearrange("p s x -> p x s"))
+
+        def quantize_t(z0, n):
+            g = z0 // ZG
+            lo = z0 % ZG
+            cols = slice(lo * P, (lo + n) * P)
+            nc.vector.quantize_mx(
+                out=t_codes[g][:, cols].bitcast(FP8X4),
+                scales=t_scales[g][:, cols],
+                in_=t_grps[g][:, lo : lo + n].rearrange("p z x s -> p (z x s)"),
+            )
+
+        def stage2(z):
+            g = z // ZG
+            if z % ZG == 0:
+                banks2[g] = ps2.tile([P, ZG, P], F32, name="bank2")
+            cols = slice((z % ZG) * P, (z % ZG + 1) * P)
+            nc.tensor.matmul_mx(
+                out=banks2[g][:, z % ZG, :],
+                lhsT=t_codes[g][:, cols].bitcast(FP8X4),
+                lhsT_scale=t_scales[g][:, cols],
+                rhs=y_codes[:].bitcast(FP8X4),
+                rhs_scale=y_scales[:],
+                start=True,
+                stop=True,
+            )
+
+        def read2(g, y0, y1):
+            dst = out_sb[:, y0:y1, g * ZG : (g + 1) * ZG]
+            src = banks2[g][:, :, y0:y1].rearrange("p z y -> p y z")
+            if g in R2_ON_V:
+                nc.vector.tensor_copy(out=dst, in_=src)
+            else:
+                nc.scalar.copy(out=dst, in_=src)
+
+        out_flat = out[0].rearrange("x y z -> x (y z)")
+        sb_flat = out_sb[:].rearrange("p y z -> p (y z)")
+        last_g = Z // ZG - 1
+
+        for k in range(Z + 6):
+            if k < Z:
+                interleave(k)
+            if k == 0:
+                nc.vector.quantize_mx(
+                    out=x_codes[:].bitcast(FP8X4), scales=x_scales[:], in_=x_grp[:].rearrange("p r t -> p (r t)")
+                )
+                nc.vector.quantize_mx(
+                    out=y_codes[:].bitcast(FP8X4), scales=y_scales[:], in_=y_grp[:].rearrange("p r t -> p (r t)")
+                )
+            if 1 <= k <= Z:
+                quantize_w(k - 1)
+                stage1(k - 1)
+            if 2 <= k <= Z + 1:
+                read1(k - 2)
+            for z0, n in PIECES:
+                if k == z0 + n - 1 + 3:
+                    quantize_t(z0, n)
+                    for z in range(z0, z0 + n):
+                        stage2(z)
+            for g in range(last_g):
+                if k == ZG * g + ZG - 1 + (5 if g in R2_ON_V else 4):
+                    read2(g, 0, P)
+            if k == Z - 1 + 4:
+                for c in range(len(Y_CUTS) - 1):
+                    read2(last_g, Y_CUTS[c], Y_CUTS[c + 1])
+                    nc.sync.dma_start(
+                        out=out_flat[:, Y_CUTS[c] * Z : Y_CUTS[c + 1] * Z], in_=sb_flat[:, Y_CUTS[c] * Z : Y_CUTS[c + 1] * Z]
+                    )

@@ -89,8 +89,8 @@ def tile_span2oscorer_pa_kernel(tc, xp, yp, w, out):
         def interleave(z):
             g = grp.tile([P, 4 * K], BF16, name="w_grp", align_bytes=64)
             w_grps[z] = g
-            dst = g[:].rearrange("p (s a i t) -> p a s i t", s=4, a=32, i=4, t=4)
-            src = raws[z][:].rearrange("p t (a s i) -> p a s i t", a=32, s=4, i=4)
+            dst = g[:].rearrange("p (s a i t) -> p a s t i", s=4, a=32, i=4, t=4)
+            src = raws[z][:].rearrange("p t (a s i) -> p a s t i", a=32, s=4, i=4)
             nc.scalar.copy(out=dst[:, A_V:32], in_=src[:, A_V:32])
             nc.vector.tensor_copy(out=dst[:, 0:A_V], in_=src[:, 0:A_V])
 

@@ -18,7 +18,7 @@ BANK_DT = F32
 FLOPS = 2 * P * K * K * Z + 2 * P * P * K * Z
 
 A_V = 20
-R2_ON_V = (6,)
+EARLY_GROUPS = (0, 1, 2)
 PIECES = [(ZG * g, ZG) for g in range(Z // ZG - 1)] + [(28, 2), (30, 1), (31, 1)]
 Y_CUTS = (0, 32, 64, 96, 128)
 
@@ -31,9 +31,8 @@ def tile_span2oscorer_pa_kernel(tc, xp, yp, w, out):
         grp = ctx.enter_context(tc.tile_pool(name="grp", bufs=3))
         wq = ctx.enter_context(tc.tile_pool(name="wq", bufs=3))
         tq = ctx.enter_context(tc.tile_pool(name="tq", bufs=2))
-        ps_head = ctx.enter_context(tc.psum_pool(name="ps_head", bufs=2))
         ps1 = ctx.enter_context(tc.psum_pool(name="ps1", bufs=3))
-        ps2 = ctx.enter_context(tc.psum_pool(name="ps2", bufs=2))
+        ps2 = ctx.enter_context(tc.psum_pool(name="ps2", bufs=5))
         ctx.enter_context(tc.manual_schedule())
 
         x_sb = const.tile([P, K + 8], BF16, name="x_sb")
@@ -65,11 +64,13 @@ def tile_span2oscorer_pa_kernel(tc, xp, yp, w, out):
         )
         x_grp = const.tile([P, P, 4], BF16, name="x_grp", align_bytes=64)
         y_grp = const.tile([P, P, 4], BF16, name="y_grp", align_bytes=64)
-        for slot, grouped in ((x_slot, x_grp), (y_slot, y_grp)):
-            turned = ps_head.tile([P, 4, P], BF16, name="turned")
-            for t in range(4):
-                nc.tensor.transpose(turned[:, t, :], slot[:, t, :], ident[:])
-            nc.scalar.copy(out=grouped[:], in_=turned[:].rearrange("p t r -> p r t"))
+        turned_x = ps2.tile([P, 4, P], BF16, name="turned_x", tag="bank2")
+        turned_y = ps2.tile([P, 4, P], BF16, name="turned_y", tag="bank2")
+        for t in range(4):
+            nc.tensor.transpose(turned_x[:, t, :], x_slot[:, t, :], ident[:])
+        for t in range(4):
+            nc.tensor.transpose(turned_y[:, t, :], y_slot[:, t, :], ident[:])
+        nc.scalar.copy(out=x_grp[:], in_=turned_x[:].rearrange("p t r -> p r t"))
         x_codes = const.tile([P, P], U32, name="x_codes", align_bytes=64)
         x_scales = const.tile([P, P], U8, name="x_scales", align_bytes=64)
         y_codes = const.tile([P, P], U32, name="y_codes", align_bytes=64)
@@ -137,7 +138,7 @@ def tile_span2oscorer_pa_kernel(tc, xp, yp, w, out):
         def stage2(z):
             g = z // ZG
             if z % ZG == 0:
-                banks2[g] = ps2.tile([P, ZG, P], F32, name="bank2")
+                banks2[g] = ps2.tile([P, ZG, P], F32, name="bank2", tag="bank2")
             cols = slice((z % ZG) * P, (z % ZG + 1) * P)
             nc.tensor.matmul_mx(
                 out=banks2[g][:, z % ZG, :],
@@ -149,44 +150,55 @@ def tile_span2oscorer_pa_kernel(tc, xp, yp, w, out):
                 stop=True,
             )
 
-        def read2(g, y0, y1):
+        def read2(engine_copy, g, y0, y1):
             dst = out_sb[:, y0:y1, g * ZG : (g + 1) * ZG]
             src = banks2[g][:, :, y0:y1].rearrange("p z y -> p y z")
-            if g in R2_ON_V:
-                nc.vector.tensor_copy(out=dst, in_=src)
-            else:
-                nc.scalar.copy(out=dst, in_=src)
+            engine_copy(out=dst, in_=src)
 
         out_flat = out[0].rearrange("x y z -> x (y z)")
         sb_flat = out_sb[:].rearrange("p y z -> p (y z)")
         last_g = Z // ZG - 1
 
-        for k in range(Z + 6):
-            if k < Z:
-                interleave(k)
+        def quantize_and_stage2(z0, n):
+            quantize_t(z0, n)
+            for z in range(z0, z0 + n):
+                stage2(z)
+
+        for k in range(Z):
+            interleave(k)
             if k == 0:
+                nc.vector.tensor_copy(out=y_grp[:], in_=turned_y[:].rearrange("p t r -> p r t"))
                 nc.vector.quantize_mx(
                     out=x_codes[:].bitcast(FP8X4), scales=x_scales[:], in_=x_grp[:].rearrange("p r t -> p (r t)")
                 )
                 nc.vector.quantize_mx(
                     out=y_codes[:].bitcast(FP8X4), scales=y_scales[:], in_=y_grp[:].rearrange("p r t -> p (r t)")
                 )
-            if 1 <= k <= Z:
+            if k >= 1:
                 quantize_w(k - 1)
                 stage1(k - 1)
-            if 2 <= k <= Z + 1:
+            if k >= 2:
                 read1(k - 2)
             for z0, n in PIECES:
                 if k == z0 + n - 1 + 3:
-                    quantize_t(z0, n)
-                    for z in range(z0, z0 + n):
-                        stage2(z)
-            for g in range(last_g):
-                if k == ZG * g + ZG - 1 + (5 if g in R2_ON_V else 4):
-                    read2(g, 0, P)
-            if k == Z - 1 + 4:
-                for c in range(len(Y_CUTS) - 1):
-                    read2(last_g, Y_CUTS[c], Y_CUTS[c + 1])
-                    nc.sync.dma_start(
-                        out=out_flat[:, Y_CUTS[c] * Z : Y_CUTS[c + 1] * Z], in_=sb_flat[:, Y_CUTS[c] * Z : Y_CUTS[c + 1] * Z]
-                    )
+                    quantize_and_stage2(z0, n)
+            for g in EARLY_GROUPS:
+                if k == ZG * g + ZG - 1 + 4:
+                    read2(nc.scalar.copy, g, 0, P)
+
+        quantize_w(Z - 1)
+        stage1(Z - 1)
+        read2(nc.scalar.copy, 3, 0, P)
+        read1(Z - 2)
+        quantize_and_stage2(28, 2)
+        read2(nc.vector.tensor_copy, 5, 0, P)
+        read1(Z - 1)
+        quantize_and_stage2(30, 1)
+        read2(nc.scalar.copy, 4, 0, P)
+        quantize_and_stage2(31, 1)
+        read2(nc.vector.tensor_copy, 6, 0, P)
+        for c in range(len(Y_CUTS) - 1):
+            read2(nc.scalar.copy, last_g, Y_CUTS[c], Y_CUTS[c + 1])
+            nc.sync.dma_start(
+                out=out_flat[:, Y_CUTS[c] * Z : Y_CUTS[c + 1] * Z], in_=sb_flat[:, Y_CUTS[c] * Z : Y_CUTS[c + 1] * Z]
+            )

from contextlib import ExitStack

import concourse.mybir as mybir
from concourse.masks import make_identity

F32 = mybir.dt.float32
BF16 = mybir.dt.bfloat16
U32 = mybir.dt.uint32
U8 = mybir.dt.uint8
FP8X4 = mybir.dt.float8_e4m3fn_x4

P = 128
K = 512
Z = 32
ZG = 4
BANK_DT = F32

FLOPS = 2 * P * K * K * Z + 2 * P * P * K * Z

A_V = 20
EARLY_GROUPS = (0, 1, 2)
PIECES = [(ZG * g, ZG) for g in range(Z // ZG - 1)] + [(28, 2), (30, 1), (31, 1)]
Y_CUTS = (0, 32, 64, 96, 128)


def tile_span2oscorer_pa_kernel(tc, xp, yp, w, out):
    nc = tc.nc
    with ExitStack() as ctx:
        const = ctx.enter_context(tc.tile_pool(name="const", bufs=1))
        rawp = ctx.enter_context(tc.tile_pool(name="rawp", bufs=Z))
        grp = ctx.enter_context(tc.tile_pool(name="grp", bufs=3))
        wq = ctx.enter_context(tc.tile_pool(name="wq", bufs=3))
        tq = ctx.enter_context(tc.tile_pool(name="tq", bufs=2))
        ps1 = ctx.enter_context(tc.psum_pool(name="ps1", bufs=3))
        ps2 = ctx.enter_context(tc.psum_pool(name="ps2", bufs=5))
        ctx.enter_context(tc.manual_schedule())

        x_sb = const.tile([P, K + 8], BF16, name="x_sb")
        y_sb = const.tile([P, K + 8], BF16, name="y_sb")
        nc.sync.dma_start(out=x_sb[:, 1:K], in_=xp[0])
        nc.sync.dma_start(out=y_sb[:, 1:K], in_=yp[0])
        nc.vector.memset(x_sb[:, K : K + 8], 1.0)
        nc.vector.memset(y_sb[:, K : K + 8], 1.0)
        raws = []
        for z in range(Z):
            raw = rawp.tile([P, 4, K], BF16, name="raw")
            src = w[0, z].rearrange("(p t) j -> p t j", t=4)
            if z < 1:
                nc.sync.dma_start(out=raw[:, :, 0 : 16 * A_V], in_=src[:, :, 0 : 16 * A_V])
                nc.sync.dma_start(out=raw[:, :, 16 * A_V : K], in_=src[:, :, 16 * A_V : K])
            else:
                nc.sync.dma_start(out=raw[:], in_=src)
            raws.append(raw)

        ident = const.tile([P, P], BF16, name="ident")
        make_identity(nc, ident[:])

        x_slot = const.tile([P, 4, P], BF16, name="x_slot")
        y_slot = const.tile([P, 4, P], BF16, name="y_slot")
        nc.vector.tensor_copy(out=x_slot[:], in_=x_sb[:, 1 : K + 1].rearrange("r (p t) -> r t p", t=4))
        nc.vector.tensor_copy(
            out=y_slot[:].rearrange("r s (a i) -> r s a i", i=4),
            in_=y_sb[:, 1 : K + 1].rearrange("r (a s i) -> r s a i", s=4, i=4),
        )
        x_grp = const.tile([P, P, 4], BF16, name="x_grp", align_bytes=64)
        y_grp = const.tile([P, P, 4], BF16, name="y_grp", align_bytes=64)
        turned_x = ps2.tile([P, 4, P], BF16, name="turned_x", tag="bank2")
        turned_y = ps2.tile([P, 4, P], BF16, name="turned_y", tag="bank2")
        for t in range(4):
            nc.tensor.transpose(turned_x[:, t, :], x_slot[:, t, :], ident[:])
        for t in range(4):
            nc.tensor.transpose(turned_y[:, t, :], y_slot[:, t, :], ident[:])
        nc.scalar.copy(out=x_grp[:], in_=turned_x[:].rearrange("p t r -> p r t"))
        x_codes = const.tile([P, P], U32, name="x_codes", align_bytes=64)
        x_scales = const.tile([P, P], U8, name="x_scales", align_bytes=64)
        y_codes = const.tile([P, P], U32, name="y_codes", align_bytes=64)
        y_scales = const.tile([P, P], U8, name="y_scales", align_bytes=64)

        out_sb = const.tile([P, P, Z], F32, name="out_sb")

        w_grps = {}
        w_codes = {}
        w_scales = {}
        banks1 = {}
        t_grps = {}
        t_codes = {}
        t_scales = {}
        banks2 = {}

        def interleave(z):
            g = grp.tile([P, 4 * K], BF16, name="w_grp", align_bytes=64)
            w_grps[z] = g
            dst = g[:].rearrange("p (s a i t) -> p a s t i", s=4, a=32, i=4, t=4)
            src = raws[z][:].rearrange("p t (a s i) -> p a s t i", a=32, s=4, i=4)
            nc.scalar.copy(out=dst[:, A_V:32], in_=src[:, A_V:32])
            nc.vector.tensor_copy(out=dst[:, 0:A_V], in_=src[:, 0:A_V])

        def quantize_w(z):
            c = wq.tile([P, K], U32, name="w_code", align_bytes=64)
            s = wq.tile([P, K], U8, name="w_scale", align_bytes=64)
            w_codes[z] = c
            w_scales[z] = s
            nc.vector.quantize_mx(out=c[:].bitcast(FP8X4), scales=s[:], in_=w_grps[z][:])

        def stage1(z):
            b = ps1.tile([P, 4, P], BANK_DT, name="bank1")
            banks1[z] = b
            for s in range(4):
                cols = slice(s * P, (s + 1) * P)
                nc.tensor.matmul_mx(
                    out=b[:, s, :],
                    lhsT=w_codes[z][:, cols].bitcast(FP8X4),
                    lhsT_scale=w_scales[z][:, cols],
                    rhs=x_codes[:].bitcast(FP8X4),
                    rhs_scale=x_scales[:],
                    start=True,
                    stop=True,
                )

        def read1(z):
            g = z // ZG
            if z % ZG == 0:
                t_grps[g] = tq.tile([P, ZG, P, 4], BF16, name="t_grp", align_bytes=64)
                t_codes[g] = tq.tile([P, ZG * P], U32, name="t_code", align_bytes=64)
                t_scales[g] = tq.tile([P, ZG * P], U8, name="t_scale", align_bytes=64)
            nc.scalar.copy(out=t_grps[g][:, z % ZG], in_=banks1[z][:].rearrange("p s x -> p x s"))

        def quantize_t(z0, n):
            g = z0 // ZG
            lo = z0 % ZG
            cols = slice(lo * P, (lo + n) * P)
            nc.vector.quantize_mx(
                out=t_codes[g][:, cols].bitcast(FP8X4),
                scales=t_scales[g][:, cols],
                in_=t_grps[g][:, lo : lo + n].rearrange("p z x s -> p (z x s)"),
            )

        def stage2(z):
            g = z // ZG
            if z % ZG == 0:
                banks2[g] = ps2.tile([P, ZG, P], F32, name="bank2", tag="bank2")
            cols = slice((z % ZG) * P, (z % ZG + 1) * P)
            nc.tensor.matmul_mx(
                out=banks2[g][:, z % ZG, :],
                lhsT=t_codes[g][:, cols].bitcast(FP8X4),
                lhsT_scale=t_scales[g][:, cols],
                rhs=y_codes[:].bitcast(FP8X4),
                rhs_scale=y_scales[:],
                start=True,
                stop=True,
            )

        def read2(engine_copy, g, y0, y1):
            dst = out_sb[:, y0:y1, g * ZG : (g + 1) * ZG]
            src = banks2[g][:, :, y0:y1].rearrange("p z y -> p y z")
            engine_copy(out=dst, in_=src)

        out_flat = out[0].rearrange("x y z -> x (y z)")
        sb_flat = out_sb[:].rearrange("p y z -> p (y z)")
        last_g = Z // ZG - 1

        def quantize_and_stage2(z0, n):
            quantize_t(z0, n)
            for z in range(z0, z0 + n):
                stage2(z)

        for k in range(Z):
            interleave(k)
            if k == 0:
                nc.vector.tensor_copy(out=y_grp[:], in_=turned_y[:].rearrange("p t r -> p r t"))
                nc.vector.quantize_mx(
                    out=x_codes[:].bitcast(FP8X4), scales=x_scales[:], in_=x_grp[:].rearrange("p r t -> p (r t)")
                )
                nc.vector.quantize_mx(
                    out=y_codes[:].bitcast(FP8X4), scales=y_scales[:], in_=y_grp[:].rearrange("p r t -> p (r t)")
                )
            if k >= 1:
                quantize_w(k - 1)
                stage1(k - 1)
            if k >= 2:
                read1(k - 2)
            for z0, n in PIECES:
                if k == z0 + n - 1 + 3:
                    quantize_and_stage2(z0, n)
            for g in EARLY_GROUPS:
                if k == ZG * g + ZG - 1 + 4:
                    read2(nc.scalar.copy, g, 0, P)

        quantize_w(Z - 1)
        stage1(Z - 1)
        read2(nc.scalar.copy, 3, 0, P)
        read1(Z - 2)
        quantize_and_stage2(28, 2)
        read2(nc.vector.tensor_copy, 5, 0, P)
        read1(Z - 1)
        quantize_and_stage2(30, 1)
        read2(nc.scalar.copy, 4, 0, P)
        quantize_and_stage2(31, 1)
        read2(nc.vector.tensor_copy, 6, 0, P)
        for c in range(len(Y_CUTS) - 1):
            read2(nc.scalar.copy, last_g, Y_CUTS[c], Y_CUTS[c + 1])
            nc.sync.dma_start(
                out=out_flat[:, Y_CUTS[c] * Z : Y_CUTS[c + 1] * Z], in_=sb_flat[:, Y_CUTS[c] * Z : Y_CUTS[c + 1] * Z]
            )
